import numpy as np
import ml_dtypes


def mxq(x, axis, fmt="e4m3"):
    dtype, down = {"e4m3": (ml_dtypes.float8_e4m3fn, 7), "e5m2": (ml_dtypes.float8_e5m2, 14)}[fmt]
    v = np.moveaxis(np.asarray(x, np.float32).astype(ml_dtypes.bfloat16).astype(np.float64), axis, -1)
    blocks = v.reshape(v.shape[:-1] + (-1, 32))
    amax = np.abs(blocks).max(-1, keepdims=True)
    byte = np.maximum(np.where(amax > 0, np.frexp(amax)[1] - 1 + 127, 0) - down, 1)
    scale = np.exp2(byte - 127.0)
    codes = (blocks / scale).astype(np.float32).astype(dtype).astype(np.float64)
    return np.moveaxis((codes * scale).reshape(v.shape), -1, axis)


WIDE = False


def mx_kscale(k):
    if not WIDE:
        return np.ones(k)
    levels = np.array([10, -10, 5, -5, 0])
    a = np.random.permutation(np.resize(levels, k // 512 * 4)).reshape(k // 512, 4)
    idx = np.arange(k)
    return np.exp2(a[idx // 512, idx % 128 // 32])


BF16 = ml_dtypes.bfloat16


def bf(x):
    return np.asarray(x, np.float32).astype(BF16)


def f64(x):
    return np.asarray(x).astype(np.float64)


B, S, D, H, DH, F = 4, 1024, 1024, 4, 128, 512
E = H * DH
EPS = 1e-5
NTERMS = 120


def layernorm(x, g, b):
    mu = x.mean(-1, keepdims=True)
    var = np.square(x - mu).mean(-1, keepdims=True)
    return (x - mu) / np.sqrt(var + EPS) * g + b


def erf(v):
    a = np.minimum(np.maximum(v, -6.0), 6.0)
    term = a.copy()
    total = a.copy()
    for n in range(1, NTERMS):
        term = term * (2.0 * a * a) / (2.0 * n + 1.0)
        total = total + term
    return 2.0 / np.sqrt(np.pi) * np.exp(-a * a) * total


def gelu_erf(v):
    return 0.5 * v * (1.0 + erf(v / np.sqrt(2.0)))


def setup_inputs():
    s, t = mx_kscale(E), mx_kscale(D)
    x = np.random.standard_normal((B, S, D)) + 0.5 * np.random.standard_normal((B, S, 1))
    return {"h_attn": bf(0.2 * np.random.standard_normal((B, S, E)) * s),
            "x": bf(x),
            "w_out": bf(np.random.standard_normal((D, E)) * 2.0 / np.sqrt(E) / s),
            "w_fc1": bf(np.random.standard_normal((F, D)) / np.sqrt(D) / t),
            "g2": bf((1.0 + 0.1 * np.random.standard_normal(D)) * t),
            "b2": bf(0.1 * np.random.standard_normal(D) * t)}


def reference(h_attn, x, w_out, w_fc1, g2, b2):
    x_mid = f64(x) + (mxq(f64(h_attn), 2, "e4m3") @ mxq(f64(w_out), 1, "e4m3").T)
    h = layernorm(x_mid, f64(g2), f64(b2))
    u = mxq(h, 2, "e4m3") @ mxq(f64(w_fc1), 1, "e4m3").T
    return x_mid, gelu_erf(u)

@@ -1,0 +1,294 @@
+from contextlib import ExitStack
+
+import concourse.mybir as mybir
+from concourse.masks import make_identity
+
+F32 = mybir.dt.float32
+BF16 = mybir.dt.bfloat16
+U32 = mybir.dt.uint32
+U8 = mybir.dt.uint8
+FP8X4 = mybir.dt.float8_e4m3fn_x4
+ACT = mybir.ActivationFunctionType
+ALU = mybir.AluOpType
+
+P = 128
+TOKENS = 4096
+D = 1024
+E = 512
+F = 512
+EPS = 1e-5
+TILES = 4
+GROUP = TILES * P
+GROUPS = TOKENS // GROUP
+BANK = 512
+D_BLOCKS = D // P
+PASSES2 = D // 512
+
+FLOPS = 2 * TOKENS * E * D + 2 * TOKENS * D * F
+
+
+def tile_minitransformerlayer_pb_t_kernel(tc, h_attn, x, w_out, w_fc1, g2, b2, out_0, out_1):
+    nc = tc.nc
+    ha_rows = h_attn.flatten_outer_dims()
+    x_rows = x.flatten_outer_dims()
+    xmid_rows = out_0.flatten_outer_dims()
+    act_rows = out_1.flatten_outer_dims()
+
+    with ExitStack() as ctx:
+        const = ctx.enter_context(tc.tile_pool(name="const", bufs=1))
+        loads = ctx.enter_context(tc.tile_pool(name="loads", bufs=3))
+        work = ctx.enter_context(tc.tile_pool(name="work", bufs=2))
+        small = ctx.enter_context(tc.tile_pool(name="small", bufs=3))
+        tp = ctx.enter_context(tc.psum_pool(name="tp", bufs=3))
+        s1p = ctx.enter_context(tc.psum_pool(name="s1p", bufs=3))
+        s2p = ctx.enter_context(tc.psum_pool(name="s2p", bufs=2))
+
+        def group_view(rows, g):
+            return rows[g * GROUP : (g + 1) * GROUP, :].rearrange("(p j) c -> p j c", j=TILES)
+
+        ha_tiles = {}
+        x_tiles = {}
+
+        def load(g):
+            ha_sb = loads.tile([P, TILES, E], BF16, name="ha_sb")
+            nc.sync.dma_start(out=ha_sb[:], in_=group_view(ha_rows, g))
+            x_sb = loads.tile([P, TILES, D], BF16, name="x_sb")
+            nc.sync.dma_start(out=x_sb[:], in_=group_view(x_rows, g))
+            ha_tiles[g] = ha_sb
+            x_tiles[g] = x_sb
+
+        w1_raw = const.tile([P, D_BLOCKS * E], BF16)
+        nc.sync.dma_start(
+            out=w1_raw[:].rearrange("p (r k) -> p r k", k=E),
+            in_=w_out.rearrange("(r p) k -> p r k", p=P),
+        )
+        load(0)
+        warm = const.tile([P, 1], F32)
+        nc.vector.memset(warm[:], 0.0)
+        nc.scalar.activation(out=warm[:], in_=warm[:], func=ACT.Gelu)
+        gb_rows = const.tile([P, P], BF16)
+        nc.vector.memset(gb_rows[:], 0.0)
+        nc.sync.dma_start(out=gb_rows[0:D_BLOCKS, :], in_=g2.rearrange("(c p) -> c p", p=P))
+        nc.sync.dma_start(out=gb_rows[D_BLOCKS : 2 * D_BLOCKS, :], in_=b2.rearrange("(c p) -> c p", p=P))
+        w2_raw = const.tile([P, F // P, D], BF16)
+        nc.sync.dma_start(out=w2_raw[:], in_=w_fc1.rearrange("(r p) k -> p r k", p=P))
+        load(1)
+
+        ident_f32 = const.tile([P, P], F32)
+        make_identity(nc, ident_f32[:])
+        ident_bf = const.tile([P, P], BF16)
+        make_identity(nc, ident_bf[:])
+        neg_half = const.tile([P, 1], F32)
+        nc.gpsimd.memset(neg_half[:], -0.5)
+
+        w1_grp = const.tile([P, D * 4], BF16, align_bytes=64)
+        w1_grp_words = w1_grp[:].bitcast(F32).rearrange("p (d u) -> p d u", u=2)
+        w1_words = w1_raw[:].bitcast(F32)
+        for q in range(D_BLOCKS // 2):
+            w1_ps = tp.tile([P, 2, 2 * P], F32, tag="tp")
+            for rr in range(2):
+                for u in range(2):
+                    col = (2 * q + rr) * (E // 2) + u * P
+                    nc.tensor.transpose(w1_ps[:, u, rr * P : (rr + 1) * P], w1_words[:, col : col + P], ident_f32[:])
+            if q % 2 == 0:
+                nc.vector.tensor_copy(
+                    out=w1_grp_words[:, q * 2 * P : (q + 1) * 2 * P, :], in_=w1_ps[:].rearrange("p u d -> p d u")
+                )
+            else:
+                nc.scalar.copy(
+                    out=w1_grp_words[:, q * 2 * P : (q + 1) * 2 * P, :], in_=w1_ps[:].rearrange("p u d -> p d u")
+                )
+        w1_codes = const.tile([P, D], U32, align_bytes=64)
+        w1_scales = const.tile([P, D], U8, align_bytes=64)
+        nc.vector.quantize_mx(out=w1_codes[:].bitcast(FP8X4), scales=w1_scales[:], in_=w1_grp[:])
+
+        gb_ps = tp.tile([P, P], BF16, tag="tp")
+        nc.tensor.transpose(gb_ps[:], gb_rows[:], ident_bf[:])
+        gb = const.tile([P, 2 * D_BLOCKS], F32)
+        nc.vector.tensor_copy(out=gb[:], in_=gb_ps[:, 0 : 2 * D_BLOCKS])
+
+        w2_grp = const.tile([P, PASSES2, F, 4], BF16, align_bytes=64)
+        w2_codes = const.tile([P, PASSES2, F], U32, align_bytes=64)
+        w2_scales = const.tile([P, PASSES2, F], U8, align_bytes=64)
+
+        def quantise_w_fc1():
+            for s in range(PASSES2):
+                for q in range(F // P // 2):
+                    w2_ps = tp.tile([P, 4, 2 * P], BF16, tag="tp")
+                    for t in range(4):
+                        for rr in range(2):
+                            c = 4 * s + t
+                            nc.tensor.transpose(
+                                w2_ps[:, t, rr * P : (rr + 1) * P],
+                                w2_raw[:, 2 * q + rr, c * P : (c + 1) * P],
+                                ident_bf[:],
+                            )
+                    nc.scalar.copy(
+                        out=w2_grp[:, s, q * 2 * P : (q + 1) * 2 * P, :], in_=w2_ps[:].rearrange("p t f -> p f t")
+                    )
+            for s in range(PASSES2):
+                nc.vector.quantize_mx(
+                    out=w2_codes[:, s, :].bitcast(FP8X4),
+                    scales=w2_scales[:, s, :],
+                    in_=w2_grp[:, s, :, :].rearrange("p f t -> p (f t)"),
+                )
+
+        h_ops = {}
+        z_tiles = {}
+        z_ops = {}
+
+        def quantise_h_attn(g):
+            ha_words = ha_tiles[g][:].rearrange("p j k -> p (j k)").bitcast(F32)
+            h_grp = work.tile([P, GROUP * 4], BF16, align_bytes=64, name="h_grp")
+            h_grp_words = h_grp[:].bitcast(F32).rearrange("p (r u) -> p r u", u=2)
+            for q in range(TILES // 2):
+                h_ps = tp.tile([P, 2, 2 * P], F32, tag="tp")
+                for jj in range(2):
+                    for u in range(2):
+                        col = (2 * q + jj) * (E // 2) + u * P
+                        nc.tensor.transpose(h_ps[:, u, jj * P : (jj + 1) * P], ha_words[:, col : col + P], ident_f32[:])
+                nc.scalar.copy(
+                    out=h_grp_words[:, q * 2 * P : (q + 1) * 2 * P, :], in_=h_ps[:].rearrange("p u r -> p r u")
+                )
+            h_codes = work.tile([P, GROUP], U32, align_bytes=64, name="h_codes")
+            h_scales = work.tile([P, GROUP], U8, align_bytes=64, name="h_scales")
+            nc.vector.quantize_mx(out=h_codes[:].bitcast(FP8X4), scales=h_scales[:], in_=h_grp[:])
+            h_ops[g] = (h_codes, h_scales)
+
+        def first_matmul_and_norm(g):
+            h_codes, h_scales = h_ops[g]
+            x_sb = x_tiles[g]
+            xm = work.tile([P, TILES, D], F32, name="xm")
+            z = work.tile([P, TILES, D], F32, name="z")
+            sums = small.tile([P, TILES, 2], F32, name="sums")
+            neg_mu = small.tile([P, TILES], F32, name="neg_mu")
+            ssq = small.tile([P, TILES], F32, name="ssq")
+            var_eps = small.tile([P, TILES], F32, name="var_eps")
+            rstd = small.tile([P, TILES], F32, name="rstd")
+            for j in range(TILES):
+                tok = slice(j * P, (j + 1) * P)
+                for half in range(D // BANK):
+                    cols = slice(half * BANK, (half + 1) * BANK)
+                    acc1 = s1p.tile([P, BANK], F32, name="acc1")
+                    nc.tensor.matmul_mx(
+                        out=acc1[:],
+                        lhsT=h_codes[:, tok].bitcast(FP8X4),
+                        lhsT_scale=h_scales[:, tok],
+                        rhs=w1_codes[:, cols].bitcast(FP8X4),
+                        rhs_scale=w1_scales[:, cols],
+                        start=True,
+                        stop=True,
+                    )
+                    nc.vector.scalar_tensor_tensor(
+                        out=xm[:, j, cols],
+                        in0=acc1[:],
+                        scalar=1.0,
+                        in1=x_sb[:, j, cols],
+                        op0=ALU.mult,
+                        op1=ALU.add,
+                        accum_out=sums[:, j, half : half + 1],
+                    )
+                nc.vector.tensor_scalar(
+                    out=neg_mu[:, j : j + 1],
+                    in0=sums[:, j, 0:1],
+                    scalar1=sums[:, j, 1:2],
+                    scalar2=-1.0 / D,
+                    op0=ALU.add,
+                    op1=ALU.mult,
+                )
+                squares = work.tile([P, D], BF16, name="squares")
+                nc.scalar.activation(
+                    out=squares[:],
+                    in_=xm[:, j, :],
+                    func=ACT.Square,
+                    bias=neg_mu[:, j : j + 1],
+                    scale=1.0,
+                    accum_out=ssq[:, j : j + 1],
+                )
+                nc.gpsimd.tensor_scalar(
+                    out=var_eps[:, j : j + 1],
+                    in0=ssq[:, j : j + 1],
+                    scalar1=1.0 / D,
+                    scalar2=EPS,
+                    op0=ALU.mult,
+                    op1=ALU.add,
+                )
+                nc.gpsimd.tensor_tensor(
+                    out=rstd[:, j : j + 1], in0=var_eps[:, j : j + 1], in1=neg_half[:], op=ALU.pow
+                )
+                nc.gpsimd.tensor_scalar(
+                    out=z[:, j, :],
+                    in0=xm[:, j, :],
+                    scalar1=neg_mu[:, j : j + 1],
+                    scalar2=rstd[:, j : j + 1],
+                    op0=ALU.add,
+                    op1=ALU.mult,
+                )
+                if j % 2 == 1:
+                    nc.sync.dma_start(out=group_view(xmid_rows, g)[:, j - 1 : j + 1, :], in_=xm[:, j - 1 : j + 1, :])
+            z_tiles[g] = z
+
+        def quantise_h(g):
+            z = z_tiles[g]
+            planes = work.tile([P, D_BLOCKS, GROUP], BF16, name="planes")
+            for c in range(D_BLOCKS):
+                z_ps = tp.tile([P, GROUP], F32, tag="tp")
+                for j in range(TILES):
+                    nc.tensor.transpose(z_ps[:, j * P : (j + 1) * P], z[:, j, c * P : (c + 1) * P], ident_f32[:])
+                gain = gb[:, c : c + 1]
+                shift = gb[:, D_BLOCKS + c : D_BLOCKS + c + 1]
+                if c % 3 != 0:
+                    nc.scalar.activation(out=planes[:, c, :], in_=z_ps[:], func=ACT.Identity, bias=shift, scale=gain)
+                else:
+                    nc.vector.tensor_scalar(
+                        out=planes[:, c, :], in0=z_ps[:], scalar1=gain, scalar2=shift, op0=ALU.mult, op1=ALU.add
+                    )
+            z_grp = work.tile([P, PASSES2, GROUP, 4], BF16, align_bytes=64, name="z_grp")
+            z_codes = work.tile([P, PASSES2, GROUP], U32, align_bytes=64, name="z_codes")
+            z_scales = work.tile([P, PASSES2, GROUP], U8, align_bytes=64, name="z_scales")
+            for s in range(PASSES2):
+                nc.vector.tensor_copy(
+                    out=z_grp[:, s, :, :].rearrange("p (c i) t -> p c t i", i=4),
+                    in_=planes[:, 4 * s : 4 * s + 4, :].rearrange("p t (c i) -> p c t i", i=4),
+                )
+            for s in range(PASSES2):
+                nc.vector.quantize_mx(
+                    out=z_codes[:, s, :].bitcast(FP8X4),
+                    scales=z_scales[:, s, :],
+                    in_=z_grp[:, s, :, :].rearrange("p r t -> p (r t)"),
+                )
+            z_ops[g] = (z_codes, z_scales)
+
+        def second_matmul(g):
+            z_codes, z_scales = z_ops[g]
+            act = work.tile([P, TILES, F], F32, name="act")
+            for j in range(TILES):
+                tok = slice(j * P, (j + 1) * P)
+                acc2 = s2p.tile([P, F], F32, name="acc2")
+                for s in range(PASSES2):
+                    nc.tensor.matmul_mx(
+                        out=acc2[:],
+                        lhsT=z_codes[:, s, tok].bitcast(FP8X4),
+                        lhsT_scale=z_scales[:, s, tok],
+                        rhs=w2_codes[:, s, :].bitcast(FP8X4),
+                        rhs_scale=w2_scales[:, s, :],
+                        start=(s == 0),
+                        stop=(s == PASSES2 - 1),
+                    )
+                nc.scalar.activation(out=act[:, j, :], in_=acc2[:], func=ACT.Gelu)
+                if j % 2 == 1:
+                    nc.sync.dma_start(out=group_view(act_rows, g)[:, j - 1 : j + 1, :], in_=act[:, j - 1 : j + 1, :])
+
+        quantise_h_attn(0)
+        for i in range(GROUPS + 1):
+            if i + 2 < GROUPS:
+                load(i + 2)
+            if i + 1 < GROUPS:
+                quantise_h_attn(i + 1)
+            if i < GROUPS:
+                first_matmul_and_norm(i)
+            if i == 0:
+                quantise_w_fc1()
+            if i >= 1:
+                quantise_h(i - 1)
+                second_matmul(i - 1)

@@ -17,12 +17,16 @@ D = 1024
 E = 512
 F = 512
 EPS = 1e-5
-TILES = 4
-GROUP = TILES * P
-GROUPS = TOKENS // GROUP
 BANK = 512
 D_BLOCKS = D // P
 PASSES2 = D // 512
+LOAD_TILES = 4
+LOAD_TOKENS = LOAD_TILES * P
+LOADS = TOKENS // LOAD_TOKENS
+TILES = 2
+GROUP = TILES * P
+GROUPS = TOKENS // GROUP
+LOADS_AHEAD = 3
 
 FLOPS = 2 * TOKENS * E * D + 2 * TOKENS * D * F
 
@@ -35,27 +39,33 @@ def tile_minitransformerlayer_pb_t_kernel(tc, h_attn, x, w_out, w_fc1, g2, b2, o
     act_rows = out_1.flatten_outer_dims()
 
     with ExitStack() as ctx:
+        ctx.enter_context(tc.manual_schedule())
         const = ctx.enter_context(tc.tile_pool(name="const", bufs=1))
-        loads = ctx.enter_context(tc.tile_pool(name="loads", bufs=3))
+        loads = ctx.enter_context(tc.tile_pool(name="loads", bufs=LOADS_AHEAD + 1))
         work = ctx.enter_context(tc.tile_pool(name="work", bufs=2))
-        small = ctx.enter_context(tc.tile_pool(name="small", bufs=3))
-        tp = ctx.enter_context(tc.psum_pool(name="tp", bufs=3))
-        s1p = ctx.enter_context(tc.psum_pool(name="s1p", bufs=3))
-        s2p = ctx.enter_context(tc.psum_pool(name="s2p", bufs=2))
+        small = ctx.enter_context(tc.tile_pool(name="small", bufs=4))
+        s1p = ctx.enter_context(tc.psum_pool(name="s1p", bufs=4))
+        s2p = ctx.enter_context(tc.psum_pool(name="s2p", bufs=1))
+        ztp = ctx.enter_context(tc.psum_pool(name="ztp", bufs=2))
+        htp = ctx.enter_context(tc.psum_pool(name="htp", bufs=1))
 
-        def group_view(rows, g):
-            return rows[g * GROUP : (g + 1) * GROUP, :].rearrange("(p j) c -> p j c", j=TILES)
+        def load_view(rows, n):
+            return rows[n * LOAD_TOKENS : (n + 1) * LOAD_TOKENS, :].rearrange("(p j) c -> p j c", j=LOAD_TILES)
+
+        def group_view(rows, k):
+            first = (k % 2) * TILES
+            return load_view(rows, k // 2)[:, first : first + TILES, :]
 
         ha_tiles = {}
         x_tiles = {}
 
-        def load(g):
-            ha_sb = loads.tile([P, TILES, E], BF16, name="ha_sb")
-            nc.sync.dma_start(out=ha_sb[:], in_=group_view(ha_rows, g))
-            x_sb = loads.tile([P, TILES, D], BF16, name="x_sb")
-            nc.sync.dma_start(out=x_sb[:], in_=group_view(x_rows, g))
-            ha_tiles[g] = ha_sb
-            x_tiles[g] = x_sb
+        def load(n):
+            ha_sb = loads.tile([P, LOAD_TILES * E], BF16, name="ha_sb")
+            nc.sync.dma_start(out=ha_sb[:].rearrange("p (j c) -> p j c", j=LOAD_TILES), in_=load_view(ha_rows, n))
+            x_sb = loads.tile([P, LOAD_TILES, D], BF16, name="x_sb")
+            nc.sync.dma_start(out=x_sb[:], in_=load_view(x_rows, n))
+            ha_tiles[n] = ha_sb
+            x_tiles[n] = x_sb
 
         w1_raw = const.tile([P, D_BLOCKS * E], BF16)
         nc.sync.dma_start(
@@ -63,16 +73,14 @@ def tile_minitransformerlayer_pb_t_kernel(tc, h_attn, x, w_out, w_fc1, g2, b2, o
             in_=w_out.rearrange("(r p) k -> p r k", p=P),
         )
         load(0)
-        warm = const.tile([P, 1], F32)
-        nc.vector.memset(warm[:], 0.0)
-        nc.scalar.activation(out=warm[:], in_=warm[:], func=ACT.Gelu)
         gb_rows = const.tile([P, P], BF16)
         nc.vector.memset(gb_rows[:], 0.0)
         nc.sync.dma_start(out=gb_rows[0:D_BLOCKS, :], in_=g2.rearrange("(c p) -> c p", p=P))
         nc.sync.dma_start(out=gb_rows[D_BLOCKS : 2 * D_BLOCKS, :], in_=b2.rearrange("(c p) -> c p", p=P))
+        load(1)
         w2_raw = const.tile([P, F // P, D], BF16)
         nc.sync.dma_start(out=w2_raw[:], in_=w_fc1.rearrange("(r p) k -> p r k", p=P))
-        load(1)
+        load(2)
 
         ident_f32 = const.tile([P, P], F32)
         make_identity(nc, ident_f32[:])
@@ -80,215 +88,273 @@ def tile_minitransformerlayer_pb_t_kernel(tc, h_attn, x, w_out, w_fc1, g2, b2, o
         make_identity(nc, ident_bf[:])
         neg_half = const.tile([P, 1], F32)
         nc.gpsimd.memset(neg_half[:], -0.5)
+        warm = const.tile([P, 1], F32)
+        nc.vector.memset(warm[:], 0.0)
+        nc.scalar.activation(out=warm[:], in_=warm[:], func=ACT.Gelu)
 
         w1_grp = const.tile([P, D * 4], BF16, align_bytes=64)
         w1_grp_words = w1_grp[:].bitcast(F32).rearrange("p (d u) -> p d u", u=2)
         w1_words = w1_raw[:].bitcast(F32)
+        w1_codes = const.tile([P, D], U32, align_bytes=64)
+        w1_scales = const.tile([P, D], U8, align_bytes=64)
         for q in range(D_BLOCKS // 2):
-            w1_ps = tp.tile([P, 2, 2 * P], F32, tag="tp")
+            w1_ps = ztp.tile([P, 2, 2 * P], F32, tag="ztp")
             for rr in range(2):
                 for u in range(2):
                     col = (2 * q + rr) * (E // 2) + u * P
                     nc.tensor.transpose(w1_ps[:, u, rr * P : (rr + 1) * P], w1_words[:, col : col + P], ident_f32[:])
+            w1_out = w1_grp_words[:, q * 2 * P : (q + 1) * 2 * P, :]
             if q % 2 == 0:
-                nc.vector.tensor_copy(
-                    out=w1_grp_words[:, q * 2 * P : (q + 1) * 2 * P, :], in_=w1_ps[:].rearrange("p u d -> p d u")
-                )
+                nc.vector.tensor_copy(out=w1_out, in_=w1_ps[:].rearrange("p u d -> p d u"))
             else:
-                nc.scalar.copy(
-                    out=w1_grp_words[:, q * 2 * P : (q + 1) * 2 * P, :], in_=w1_ps[:].rearrange("p u d -> p d u")
-                )
-        w1_codes = const.tile([P, D], U32, align_bytes=64)
-        w1_scales = const.tile([P, D], U8, align_bytes=64)
-        nc.vector.quantize_mx(out=w1_codes[:].bitcast(FP8X4), scales=w1_scales[:], in_=w1_grp[:])
+                nc.scalar.copy(out=w1_out, in_=w1_ps[:].rearrange("p u d -> p d u"))
+        for half in range(D // BANK):
+            nc.vector.quantize_mx(
+                out=w1_codes[:, half * BANK : (half + 1) * BANK].bitcast(FP8X4),
+                scales=w1_scales[:, half * BANK : (half + 1) * BANK],
+                in_=w1_grp[:, half * BANK * 4 : (half + 1) * BANK * 4],
+            )
 
-        gb_ps = tp.tile([P, P], BF16, tag="tp")
-        nc.tensor.transpose(gb_ps[:], gb_rows[:], ident_bf[:])
         gb = const.tile([P, 2 * D_BLOCKS], F32)
-        nc.vector.tensor_copy(out=gb[:], in_=gb_ps[:, 0 : 2 * D_BLOCKS])
+
+        def transpose_gain_and_bias():
+            gb_ps = ztp.tile([P, P], BF16, tag="ztp")
+            nc.tensor.transpose(gb_ps[:], gb_rows[:], ident_bf[:])
+            nc.vector.tensor_copy(out=gb[:], in_=gb_ps[:, 0 : 2 * D_BLOCKS])
 
         w2_grp = const.tile([P, PASSES2, F, 4], BF16, align_bytes=64)
         w2_codes = const.tile([P, PASSES2, F], U32, align_bytes=64)
         w2_scales = const.tile([P, PASSES2, F], U8, align_bytes=64)
 
-        def quantise_w_fc1():
-            for s in range(PASSES2):
-                for q in range(F // P // 2):
-                    w2_ps = tp.tile([P, 4, 2 * P], BF16, tag="tp")
-                    for t in range(4):
-                        for rr in range(2):
-                            c = 4 * s + t
-                            nc.tensor.transpose(
-                                w2_ps[:, t, rr * P : (rr + 1) * P],
-                                w2_raw[:, 2 * q + rr, c * P : (c + 1) * P],
-                                ident_bf[:],
-                            )
-                    nc.scalar.copy(
-                        out=w2_grp[:, s, q * 2 * P : (q + 1) * 2 * P, :], in_=w2_ps[:].rearrange("p t f -> p f t")
-                    )
-            for s in range(PASSES2):
-                nc.vector.quantize_mx(
-                    out=w2_codes[:, s, :].bitcast(FP8X4),
-                    scales=w2_scales[:, s, :],
-                    in_=w2_grp[:, s, :, :].rearrange("p f t -> p (f t)"),
-                )
-
-        h_ops = {}
-        z_tiles = {}
-        z_ops = {}
-
-        def quantise_h_attn(g):
-            ha_words = ha_tiles[g][:].rearrange("p j k -> p (j k)").bitcast(F32)
-            h_grp = work.tile([P, GROUP * 4], BF16, align_bytes=64, name="h_grp")
-            h_grp_words = h_grp[:].bitcast(F32).rearrange("p (r u) -> p r u", u=2)
-            for q in range(TILES // 2):
-                h_ps = tp.tile([P, 2, 2 * P], F32, tag="tp")
-                for jj in range(2):
-                    for u in range(2):
-                        col = (2 * q + jj) * (E // 2) + u * P
-                        nc.tensor.transpose(h_ps[:, u, jj * P : (jj + 1) * P], ha_words[:, col : col + P], ident_f32[:])
+        def quantise_w_fc1(s):
+            for q in range(F // P // 2):
+                w2_ps = ztp.tile([P, 4, 2 * P], BF16, tag="ztp")
+                for t in range(4):
+                    for rr in range(2):
+                        c = 4 * s + t
+                        nc.tensor.transpose(
+                            w2_ps[:, t, rr * P : (rr + 1) * P], w2_raw[:, 2 * q + rr, c * P : (c + 1) * P], ident_bf[:]
+                        )
                 nc.scalar.copy(
-                    out=h_grp_words[:, q * 2 * P : (q + 1) * 2 * P, :], in_=h_ps[:].rearrange("p u r -> p r u")
+                    out=w2_grp[:, s, q * 2 * P : (q + 1) * 2 * P, :], in_=w2_ps[:].rearrange("p t f -> p f t")
                 )
-            h_codes = work.tile([P, GROUP], U32, align_bytes=64, name="h_codes")
-            h_scales = work.tile([P, GROUP], U8, align_bytes=64, name="h_scales")
-            nc.vector.quantize_mx(out=h_codes[:].bitcast(FP8X4), scales=h_scales[:], in_=h_grp[:])
-            h_ops[g] = (h_codes, h_scales)
+            nc.vector.quantize_mx(
+                out=w2_codes[:, s, :].bitcast(FP8X4),
+                scales=w2_scales[:, s, :],
+                in_=w2_grp[:, s, :, :].rearrange("p f t -> p (f t)"),
+            )
 
-        def first_matmul_and_norm(g):
-            h_codes, h_scales = h_ops[g]
-            x_sb = x_tiles[g]
-            xm = work.tile([P, TILES, D], F32, name="xm")
-            z = work.tile([P, TILES, D], F32, name="z")
-            sums = small.tile([P, TILES, 2], F32, name="sums")
-            neg_mu = small.tile([P, TILES], F32, name="neg_mu")
-            ssq = small.tile([P, TILES], F32, name="ssq")
-            var_eps = small.tile([P, TILES], F32, name="var_eps")
-            rstd = small.tile([P, TILES], F32, name="rstd")
-            for j in range(TILES):
-                tok = slice(j * P, (j + 1) * P)
-                for half in range(D // BANK):
-                    cols = slice(half * BANK, (half + 1) * BANK)
-                    acc1 = s1p.tile([P, BANK], F32, name="acc1")
-                    nc.tensor.matmul_mx(
-                        out=acc1[:],
-                        lhsT=h_codes[:, tok].bitcast(FP8X4),
-                        lhsT_scale=h_scales[:, tok],
-                        rhs=w1_codes[:, cols].bitcast(FP8X4),
-                        rhs_scale=w1_scales[:, cols],
-                        start=True,
-                        stop=True,
-                    )
-                    nc.vector.scalar_tensor_tensor(
-                        out=xm[:, j, cols],
-                        in0=acc1[:],
-                        scalar=1.0,
-                        in1=x_sb[:, j, cols],
-                        op0=ALU.mult,
-                        op1=ALU.add,
-                        accum_out=sums[:, j, half : half + 1],
-                    )
-                nc.vector.tensor_scalar(
-                    out=neg_mu[:, j : j + 1],
-                    in0=sums[:, j, 0:1],
-                    scalar1=sums[:, j, 1:2],
-                    scalar2=-1.0 / D,
-                    op0=ALU.add,
-                    op1=ALU.mult,
+        h_banks = {}
+        h_groups = {}
+        h_ops = {}
+        acc1_banks = {}
+        xm_tiles = {}
+        mean_tiles = {}
+        z_tiles = {}
+        norm_tiles = {}
+        plane_tiles = {}
+        zgrp_tiles = {}
+        z_ops = {}
+        act_tiles = {}
+
+        def live(k):
+            return 0 <= k < GROUPS
+
+        def transpose_h_attn(k, h):
+            if h == 0:
+                h_banks[k] = htp.tile([P, 2, GROUP], F32, name="h_ps")
+            h_ps = h_banks[k]
+            ha_words = ha_tiles[k // 2][:].bitcast(F32)
+            for u in range(2):
+                col = ((k % 2) * TILES + h) * (E // 2) + u * P
+                nc.tensor.transpose(h_ps[:, u, h * P : (h + 1) * P], ha_words[:, col : col + P], ident_f32[:])
+            if h == TILES - 1:
+                h_grp = work.tile([P, GROUP * 4], BF16, align_bytes=64, name="h_grp")
+                nc.scalar.copy(
+                    out=h_grp[:].bitcast(F32).rearrange("p (r u) -> p r u", u=2), in_=h_ps[:].rearrange("p u r -> p r u")
                 )
-                squares = work.tile([P, D], BF16, name="squares")
-                nc.scalar.activation(
-                    out=squares[:],
-                    in_=xm[:, j, :],
-                    func=ACT.Square,
-                    bias=neg_mu[:, j : j + 1],
-                    scale=1.0,
-                    accum_out=ssq[:, j : j + 1],
+                h_groups[k] = h_grp
+
+        def quantise_h_attn(k):
+            h_codes = work.tile([P, GROUP], U32, align_bytes=64, name="h_codes", bufs=3)
+            h_scales = work.tile([P, GROUP], U8, align_bytes=64, name="h_scales", bufs=3)
+            nc.vector.quantize_mx(out=h_codes[:].bitcast(FP8X4), scales=h_scales[:], in_=h_groups[k][:])
+            h_ops[k] = (h_codes, h_scales)
+
+        def first_matmul(k, h):
+            h_codes, h_scales = h_ops[k]
+            tok = slice(h * P, (h + 1) * P)
+            for half in range(D // BANK):
+                cols = slice(half * BANK, (half + 1) * BANK)
+                acc1 = s1p.tile([P, BANK], F32, name="acc1")
+                nc.tensor.matmul_mx(
+                    out=acc1[:],
+                    lhsT=h_codes[:, tok].bitcast(FP8X4),
+                    lhsT_scale=h_scales[:, tok],
+                    rhs=w1_codes[:, cols].bitcast(FP8X4),
+                    rhs_scale=w1_scales[:, cols],
+                    start=True,
+                    stop=True,
                 )
-                nc.gpsimd.tensor_scalar(
-                    out=var_eps[:, j : j + 1],
-                    in0=ssq[:, j : j + 1],
-                    scalar1=1.0 / D,
-                    scalar2=EPS,
+                acc1_banks[(k, h, half)] = acc1
+
+        def add_residual(k, h):
+            if h == 0:
+                xm_tiles[k] = work.tile([P, TILES, D], F32, name="xm", bufs=3)
+                mean_tiles[k] = (
+                    small.tile([P, TILES, 2], F32, name="sums"),
+                    small.tile([P, TILES], F32, name="neg_mu"),
+                )
+            xm = xm_tiles[k]
+            sums, neg_mu = mean_tiles[k]
+            x_sb = x_tiles[k // 2]
+            for half in range(D // BANK):
+                cols = slice(half * BANK, (half + 1) * BANK)
+                nc.vector.scalar_tensor_tensor(
+                    out=xm[:, h, cols],
+                    in0=acc1_banks[(k, h, half)][:],
+                    scalar=1.0,
+                    in1=x_sb[:, (k % 2) * TILES + h, cols],
                     op0=ALU.mult,
                     op1=ALU.add,
+                    accum_out=sums[:, h, half : half + 1],
                 )
-                nc.gpsimd.tensor_tensor(
-                    out=rstd[:, j : j + 1], in0=var_eps[:, j : j + 1], in1=neg_half[:], op=ALU.pow
-                )
-                nc.gpsimd.tensor_scalar(
-                    out=z[:, j, :],
-                    in0=xm[:, j, :],
-                    scalar1=neg_mu[:, j : j + 1],
-                    scalar2=rstd[:, j : j + 1],
-                    op0=ALU.add,
-                    op1=ALU.mult,
-                )
-                if j % 2 == 1:
-                    nc.sync.dma_start(out=group_view(xmid_rows, g)[:, j - 1 : j + 1, :], in_=xm[:, j - 1 : j + 1, :])
-            z_tiles[g] = z
+            nc.vector.tensor_scalar(
+                out=neg_mu[:, h : h + 1],
+                in0=sums[:, h, 0:1],
+                scalar1=sums[:, h, 1:2],
+                scalar2=-1.0 / D,
+                op0=ALU.add,
+                op1=ALU.mult,
+            )
+            if h == TILES - 1:
+                nc.sync.dma_start(out=group_view(xmid_rows, k), in_=xm[:])
 
-        def quantise_h(g):
-            z = z_tiles[g]
-            planes = work.tile([P, D_BLOCKS, GROUP], BF16, name="planes")
-            for c in range(D_BLOCKS):
-                z_ps = tp.tile([P, GROUP], F32, tag="tp")
-                for j in range(TILES):
-                    nc.tensor.transpose(z_ps[:, j * P : (j + 1) * P], z[:, j, c * P : (c + 1) * P], ident_f32[:])
-                gain = gb[:, c : c + 1]
-                shift = gb[:, D_BLOCKS + c : D_BLOCKS + c + 1]
-                if c % 3 != 0:
-                    nc.scalar.activation(out=planes[:, c, :], in_=z_ps[:], func=ACT.Identity, bias=shift, scale=gain)
-                else:
-                    nc.vector.tensor_scalar(
-                        out=planes[:, c, :], in0=z_ps[:], scalar1=gain, scalar2=shift, op0=ALU.mult, op1=ALU.add
-                    )
+        def normalise(k, h):
+            if h == 0:
+                z_tiles[k] = work.tile([P, TILES, D], F32, name="z", bufs=4)
+                norm_tiles[k] = (
+                    small.tile([P, TILES], F32, name="ssq"),
+                    small.tile([P, TILES], F32, name="var_eps"),
+                    small.tile([P, TILES], F32, name="rstd"),
+                )
+            xm = xm_tiles[k]
+            z = z_tiles[k]
+            neg_mu = mean_tiles[k][1]
+            ssq, var_eps, rstd = norm_tiles[k]
+            one = slice(h, h + 1)
+            squares = work.tile([P, D], BF16, name="squares")
+            nc.scalar.activation(
+                out=squares[:], in_=xm[:, h, :], func=ACT.Square, bias=neg_mu[:, one], scale=1.0, accum_out=ssq[:, one]
+            )
+            nc.gpsimd.tensor_scalar(
+                out=var_eps[:, one], in0=ssq[:, one], scalar1=1.0 / D, scalar2=EPS, op0=ALU.mult, op1=ALU.add
+            )
+            nc.gpsimd.tensor_tensor(out=rstd[:, one], in0=var_eps[:, one], in1=neg_half[:], op=ALU.pow)
+            nc.gpsimd.tensor_scalar(
+                out=z[:, h, :], in0=xm[:, h, :], scalar1=neg_mu[:, one], scalar2=rstd[:, one], op0=ALU.add, op1=ALU.mult
+            )
+
+        def transpose_z(k, h):
+            if h == 0:
+                plane_tiles[k] = work.tile([P, D_BLOCKS, GROUP], BF16, name="planes")
+            planes = plane_tiles[k]
+            z = z_tiles[k]
+            for b in range(2):
+                z_ps = ztp.tile([P, 2, GROUP], F32, tag="ztp")
+                for cc in range(2):
+                    c = 4 * h + 2 * b + cc
+                    for j in range(TILES):
+                        nc.tensor.transpose(z_ps[:, cc, j * P : (j + 1) * P], z[:, j, c * P : (c + 1) * P], ident_f32[:])
+                for cc in range(2):
+                    c = 4 * h + 2 * b + cc
+                    gain = gb[:, c : c + 1]
+                    shift = gb[:, D_BLOCKS + c : D_BLOCKS + c + 1]
+                    if h == 1 and b == 1:
+                        nc.vector.tensor_scalar(
+                            out=planes[:, c, :], in0=z_ps[:, cc, :], scalar1=gain, scalar2=shift, op0=ALU.mult, op1=ALU.add
+                        )
+                    else:
+                        nc.scalar.activation(
+                            out=planes[:, c, :], in_=z_ps[:, cc, :], func=ACT.Identity, bias=shift, scale=gain
+                        )
+
+        def regroup_h(k):
             z_grp = work.tile([P, PASSES2, GROUP, 4], BF16, align_bytes=64, name="z_grp")
-            z_codes = work.tile([P, PASSES2, GROUP], U32, align_bytes=64, name="z_codes")
-            z_scales = work.tile([P, PASSES2, GROUP], U8, align_bytes=64, name="z_scales")
             for s in range(PASSES2):
                 nc.vector.tensor_copy(
                     out=z_grp[:, s, :, :].rearrange("p (c i) t -> p c t i", i=4),
-                    in_=planes[:, 4 * s : 4 * s + 4, :].rearrange("p t (c i) -> p c t i", i=4),
+                    in_=plane_tiles[k][:, 4 * s : 4 * s + 4, :].rearrange("p t (c i) -> p c t i", i=4),
                 )
+            zgrp_tiles[k] = z_grp
+
+        def quantise_h(k):
+            z_codes = work.tile([P, PASSES2, GROUP], U32, align_bytes=64, name="z_codes")
+            z_scales = work.tile([P, PASSES2, GROUP], U8, align_bytes=64, name="z_scales")
+            nc.vector.quantize_mx(
+                out=z_codes[:].rearrange("p s r -> p (s r)").bitcast(FP8X4),
+                scales=z_scales[:].rearrange("p s r -> p (s r)"),
+                in_=zgrp_tiles[k][:].rearrange("p s r t -> p (s r t)"),
+            )
+            z_ops[k] = (z_codes, z_scales)
+
+        def second_matmul(k, h):
+            z_codes, z_scales = z_ops[k]
+            tok = slice(h * P, (h + 1) * P)
+            acc2 = s2p.tile([P, F], F32, name="acc2")
             for s in range(PASSES2):
-                nc.vector.quantize_mx(
-                    out=z_codes[:, s, :].bitcast(FP8X4),
-                    scales=z_scales[:, s, :],
-                    in_=z_grp[:, s, :, :].rearrange("p r t -> p (r t)"),
+                nc.tensor.matmul_mx(
+                    out=acc2[:],
+                    lhsT=z_codes[:, s, tok].bitcast(FP8X4),
+                    lhsT_scale=z_scales[:, s, tok],
+                    rhs=w2_codes[:, s, :].bitcast(FP8X4),
+                    rhs_scale=w2_scales[:, s, :],
+                    start=(s == 0),
+                    stop=(s == PASSES2 - 1),
                 )
-            z_ops[g] = (z_codes, z_scales)
+            return acc2
 
-        def second_matmul(g):
-            z_codes, z_scales = z_ops[g]
-            act = work.tile([P, TILES, F], F32, name="act")
-            for j in range(TILES):
-                tok = slice(j * P, (j + 1) * P)
-                acc2 = s2p.tile([P, F], F32, name="acc2")
-                for s in range(PASSES2):
-                    nc.tensor.matmul_mx(
-                        out=acc2[:],
-                        lhsT=z_codes[:, s, tok].bitcast(FP8X4),
-                        lhsT_scale=z_scales[:, s, tok],
-                        rhs=w2_codes[:, s, :].bitcast(FP8X4),
-                        rhs_scale=w2_scales[:, s, :],
-                        start=(s == 0),
-                        stop=(s == PASSES2 - 1),
-                    )
-                nc.scalar.activation(out=act[:, j, :], in_=acc2[:], func=ACT.Gelu)
-                if j % 2 == 1:
-                    nc.sync.dma_start(out=group_view(act_rows, g)[:, j - 1 : j + 1, :], in_=act[:, j - 1 : j + 1, :])
+        def gelu(k, h, acc2):
+            if h == 0:
+                act_tiles[k] = work.tile([P, TILES, F], F32, name="act", bufs=3)
+            act = act_tiles[k]
+            nc.scalar.activation(out=act[:, h, :], in_=acc2[:], func=ACT.Gelu)
+            if h == TILES - 1:
+                nc.sync.dma_start(out=group_view(act_rows, k), in_=act[:])
 
+        for k in range(2):
+            for h in range(TILES):
+                transpose_h_attn(k, h)
         quantise_h_attn(0)
-        for i in range(GROUPS + 1):
-            if i + 2 < GROUPS:
-                load(i + 2)
-            if i + 1 < GROUPS:
-                quantise_h_attn(i + 1)
-            if i < GROUPS:
-                first_matmul_and_norm(i)
-            if i == 0:
-                quantise_w_fc1()
-            if i >= 1:
-                quantise_h(i - 1)
-                second_matmul(i - 1)
+        first_matmul(0, 0)
+        for k in range(GROUPS + 4):
+            if k % 2 == 0 and k // 2 + LOADS_AHEAD < LOADS:
+                load(k // 2 + LOADS_AHEAD)
+            for h in range(TILES):
+                acc2 = second_matmul(k - 4, h) if live(k - 4) else None
+                after_k, after_h = (k, 1) if h == 0 else (k + 1, 0)
+                if live(after_k):
+                    first_matmul(after_k, after_h)
+                before_k, before_h = (k - 1, 1) if h == 0 else (k, 0)
+                if live(before_k):
+                    normalise(before_k, before_h)
+                if live(k):
+                    add_residual(k, h)
+                if live(k - 4):
+                    gelu(k - 4, h, acc2)
+                if h == 1 and live(k - 3):
+                    quantise_h(k - 3)
+                if live(k - 2):
+                    transpose_z(k - 2, h)
+                if h == 0 and live(k - 3):
+                    regroup_h(k - 3)
+                if h == 0 and live(k + 1):
+                    quantise_h_attn(k + 1)
+                if live(k + 2):
+                    transpose_h_attn(k + 2, h)
+                if k == 0 and h == 0:
+                    transpose_gain_and_bias()
+                if k == 0 and h == 1:
+                    quantise_w_fc1(0)
+                if k == 1 and h == 0:
+                    quantise_w_fc1(1)

@@ -230,16 +230,14 @@ def tile_minitransformerlayer_pb_t_kernel(tc, h_attn, x, w_out, w_fc1, g2, b2, o
             if h == TILES - 1:
                 nc.sync.dma_start(out=group_view(xmid_rows, k), in_=xm[:])
 
-        def normalise(k, h):
+        def variance(k, h):
             if h == 0:
-                z_tiles[k] = work.tile([P, TILES, D], F32, name="z", bufs=4)
                 norm_tiles[k] = (
                     small.tile([P, TILES], F32, name="ssq"),
                     small.tile([P, TILES], F32, name="var_eps"),
                     small.tile([P, TILES], F32, name="rstd"),
                 )
             xm = xm_tiles[k]
-            z = z_tiles[k]
             neg_mu = mean_tiles[k][1]
             ssq, var_eps, rstd = norm_tiles[k]
             one = slice(h, h + 1)
@@ -251,8 +249,18 @@ def tile_minitransformerlayer_pb_t_kernel(tc, h_attn, x, w_out, w_fc1, g2, b2, o
                 out=var_eps[:, one], in0=ssq[:, one], scalar1=1.0 / D, scalar2=EPS, op0=ALU.mult, op1=ALU.add
             )
             nc.gpsimd.tensor_tensor(out=rstd[:, one], in0=var_eps[:, one], in1=neg_half[:], op=ALU.pow)
-            nc.gpsimd.tensor_scalar(
-                out=z[:, h, :], in0=xm[:, h, :], scalar1=neg_mu[:, one], scalar2=rstd[:, one], op0=ALU.add, op1=ALU.mult
+
+        def normalise(k, h):
+            if h == 0:
+                z_tiles[k] = work.tile([P, TILES, D], F32, name="z", bufs=4)
+            one = slice(h, h + 1)
+            nc.vector.tensor_scalar(
+                out=z_tiles[k][:, h, :],
+                in0=xm_tiles[k][:, h, :],
+                scalar1=mean_tiles[k][1][:, one],
+                scalar2=norm_tiles[k][2][:, one],
+                op0=ALU.add,
+                op1=ALU.mult,
             )
 
         def transpose_z(k, h):
@@ -337,9 +345,11 @@ def tile_minitransformerlayer_pb_t_kernel(tc, h_attn, x, w_out, w_fc1, g2, b2, o
                     first_matmul(after_k, after_h)
                 before_k, before_h = (k - 1, 1) if h == 0 else (k, 0)
                 if live(before_k):
-                    normalise(before_k, before_h)
+                    variance(before_k, before_h)
                 if live(k):
                     add_residual(k, h)
+                if live(k - 1):
+                    normalise(k - 1, h)
                 if live(k - 4):
                     gelu(k - 4, h, acc2)
                 if h == 1 and live(k - 3):

@@ -43,7 +43,7 @@ def tile_minitransformerlayer_pb_t_kernel(tc, h_attn, x, w_out, w_fc1, g2, b2, o
         const = ctx.enter_context(tc.tile_pool(name="const", bufs=1))
         loads = ctx.enter_context(tc.tile_pool(name="loads", bufs=LOADS_AHEAD + 1))
         work = ctx.enter_context(tc.tile_pool(name="work", bufs=2))
-        small = ctx.enter_context(tc.tile_pool(name="small", bufs=4))
+        small = ctx.enter_context(tc.tile_pool(name="small", bufs=6))
         s1p = ctx.enter_context(tc.psum_pool(name="s1p", bufs=4))
         s2p = ctx.enter_context(tc.psum_pool(name="s2p", bufs=1))
         ztp = ctx.enter_context(tc.psum_pool(name="ztp", bufs=2))
@@ -59,34 +59,40 @@ def tile_minitransformerlayer_pb_t_kernel(tc, h_attn, x, w_out, w_fc1, g2, b2, o
         ha_tiles = {}
         x_tiles = {}
 
-        def load(n):
+        def load_h_attn(n):
             ha_sb = loads.tile([P, LOAD_TILES * E], BF16, name="ha_sb")
             nc.sync.dma_start(out=ha_sb[:].rearrange("p (j c) -> p j c", j=LOAD_TILES), in_=load_view(ha_rows, n))
+            ha_tiles[n] = ha_sb
+
+        def load_x(n):
             x_sb = loads.tile([P, LOAD_TILES, D], BF16, name="x_sb")
             nc.sync.dma_start(out=x_sb[:], in_=load_view(x_rows, n))
-            ha_tiles[n] = ha_sb
             x_tiles[n] = x_sb
 
+        load_h_attn(0)
         w1_raw = const.tile([P, D_BLOCKS * E], BF16)
-        nc.sync.dma_start(
-            out=w1_raw[:].rearrange("p (r k) -> p r k", k=E),
-            in_=w_out.rearrange("(r p) k -> p r k", p=P),
-        )
-        load(0)
+        w1_raw_blocks = w1_raw[:].rearrange("p (r k) -> p r k", k=E)
+        w_out_blocks = w_out.rearrange("(r p) k -> p r k", p=P)
+        for half in range(D // BANK):
+            blocks = slice(half * BANK // P, (half + 1) * BANK // P)
+            nc.sync.dma_start(out=w1_raw_blocks[:, blocks, :], in_=w_out_blocks[:, blocks, :])
+        load_x(0)
+        load_h_attn(1)
         gb_rows = const.tile([P, P], BF16)
         nc.vector.memset(gb_rows[:], 0.0)
         nc.sync.dma_start(out=gb_rows[0:D_BLOCKS, :], in_=g2.rearrange("(c p) -> c p", p=P))
         nc.sync.dma_start(out=gb_rows[D_BLOCKS : 2 * D_BLOCKS, :], in_=b2.rearrange("(c p) -> c p", p=P))
-        load(1)
         w2_raw = const.tile([P, F // P, D], BF16)
         nc.sync.dma_start(out=w2_raw[:], in_=w_fc1.rearrange("(r p) k -> p r k", p=P))
-        load(2)
+        load_x(1)
+        load_h_attn(2)
+        load_x(2)
 
         ident_f32 = const.tile([P, P], F32)
         make_identity(nc, ident_f32[:])
         ident_bf = const.tile([P, P], BF16)
         make_identity(nc, ident_bf[:])
-        neg_half = const.tile([P, 1], F32)
+        neg_half = const.tile([P, TILES], F32)
         nc.gpsimd.memset(neg_half[:], -0.5)
         warm = const.tile([P, 1], F32)
         nc.vector.memset(warm[:], 0.0)
@@ -97,23 +103,25 @@ def tile_minitransformerlayer_pb_t_kernel(tc, h_attn, x, w_out, w_fc1, g2, b2, o
         w1_words = w1_raw[:].bitcast(F32)
         w1_codes = const.tile([P, D], U32, align_bytes=64)
         w1_scales = const.tile([P, D], U8, align_bytes=64)
-        for q in range(D_BLOCKS // 2):
-            w1_ps = ztp.tile([P, 2, 2 * P], F32, tag="ztp")
-            for rr in range(2):
-                for u in range(2):
-                    col = (2 * q + rr) * (E // 2) + u * P
-                    nc.tensor.transpose(w1_ps[:, u, rr * P : (rr + 1) * P], w1_words[:, col : col + P], ident_f32[:])
-            w1_out = w1_grp_words[:, q * 2 * P : (q + 1) * 2 * P, :]
-            if q % 2 == 0:
-                nc.vector.tensor_copy(out=w1_out, in_=w1_ps[:].rearrange("p u d -> p d u"))
-            else:
-                nc.scalar.copy(out=w1_out, in_=w1_ps[:].rearrange("p u d -> p d u"))
-        for half in range(D // BANK):
-            nc.vector.quantize_mx(
-                out=w1_codes[:, half * BANK : (half + 1) * BANK].bitcast(FP8X4),
-                scales=w1_scales[:, half * BANK : (half + 1) * BANK],
-                in_=w1_grp[:, half * BANK * 4 : (half + 1) * BANK * 4],
-            )
+
+        def quantise_w_out():
+            for q in range(D_BLOCKS // 2):
+                w1_ps = ztp.tile([P, 2, 2 * P], F32, tag="ztp")
+                for rr in range(2):
+                    for u in range(2):
+                        col = (2 * q + rr) * (E // 2) + u * P
+                        nc.tensor.transpose(w1_ps[:, u, rr * P : (rr + 1) * P], w1_words[:, col : col + P], ident_f32[:])
+                w1_out = w1_grp_words[:, q * 2 * P : (q + 1) * 2 * P, :]
+                if q % 2 == 0:
+                    nc.vector.tensor_copy(out=w1_out, in_=w1_ps[:].rearrange("p u d -> p d u"))
+                else:
+                    nc.scalar.copy(out=w1_out, in_=w1_ps[:].rearrange("p u d -> p d u"))
+                    half = q // 2
+                    nc.vector.quantize_mx(
+                        out=w1_codes[:, half * BANK : (half + 1) * BANK].bitcast(FP8X4),
+                        scales=w1_scales[:, half * BANK : (half + 1) * BANK],
+                        in_=w1_grp[:, half * BANK * 4 : (half + 1) * BANK * 4],
+                    )
 
         gb = const.tile([P, 2 * D_BLOCKS], F32)
 
@@ -126,7 +134,7 @@ def tile_minitransformerlayer_pb_t_kernel(tc, h_attn, x, w_out, w_fc1, g2, b2, o
         w2_codes = const.tile([P, PASSES2, F], U32, align_bytes=64)
         w2_scales = const.tile([P, PASSES2, F], U8, align_bytes=64)
 
-        def quantise_w_fc1(s):
+        def transpose_w_fc1(s):
             for q in range(F // P // 2):
                 w2_ps = ztp.tile([P, 4, 2 * P], BF16, tag="ztp")
                 for t in range(4):
@@ -138,6 +146,8 @@ def tile_minitransformerlayer_pb_t_kernel(tc, h_attn, x, w_out, w_fc1, g2, b2, o
                 nc.scalar.copy(
                     out=w2_grp[:, s, q * 2 * P : (q + 1) * 2 * P, :], in_=w2_ps[:].rearrange("p t f -> p f t")
                 )
+
+        def quantise_w_fc1(s):
             nc.vector.quantize_mx(
                 out=w2_codes[:, s, :].bitcast(FP8X4),
                 scales=w2_scales[:, s, :],
@@ -200,7 +210,7 @@ def tile_minitransformerlayer_pb_t_kernel(tc, h_attn, x, w_out, w_fc1, g2, b2, o
 
         def add_residual(k, h):
             if h == 0:
-                xm_tiles[k] = work.tile([P, TILES, D], F32, name="xm", bufs=3)
+                xm_tiles[k] = work.tile([P, TILES, D], F32, name="xm", bufs=4)
                 mean_tiles[k] = (
                     small.tile([P, TILES, 2], F32, name="sums"),
                     small.tile([P, TILES], F32, name="neg_mu"),
@@ -245,16 +255,18 @@ def tile_minitransformerlayer_pb_t_kernel(tc, h_attn, x, w_out, w_fc1, g2, b2, o
             nc.scalar.activation(
                 out=squares[:], in_=xm[:, h, :], func=ACT.Square, bias=neg_mu[:, one], scale=1.0, accum_out=ssq[:, one]
             )
-            nc.gpsimd.tensor_scalar(
-                out=var_eps[:, one], in0=ssq[:, one], scalar1=1.0 / D, scalar2=EPS, op0=ALU.mult, op1=ALU.add
-            )
-            nc.gpsimd.tensor_tensor(out=rstd[:, one], in0=var_eps[:, one], in1=neg_half[:], op=ALU.pow)
+
+        def reciprocal_std(k):
+            ssq, var_eps, rstd = norm_tiles[k]
+            nc.vector.tensor_scalar(out=var_eps[:], in0=ssq[:], scalar1=1.0 / D, scalar2=EPS, op0=ALU.mult, op1=ALU.add)
+            nc.gpsimd.tensor_tensor(out=rstd[:], in0=var_eps[:], in1=neg_half[:], op=ALU.pow)
 
         def normalise(k, h):
             if h == 0:
                 z_tiles[k] = work.tile([P, TILES, D], F32, name="z", bufs=4)
             one = slice(h, h + 1)
-            nc.vector.tensor_scalar(
+            engine = nc.gpsimd if h == 0 else nc.vector
+            engine.tensor_scalar(
                 out=z_tiles[k][:, h, :],
                 in0=xm_tiles[k][:, h, :],
                 scalar1=mean_tiles[k][1][:, one],
@@ -330,16 +342,19 @@ def tile_minitransformerlayer_pb_t_kernel(tc, h_attn, x, w_out, w_fc1, g2, b2, o
             if h == TILES - 1:
                 nc.sync.dma_start(out=group_view(act_rows, k), in_=act[:])
 
-        for k in range(2):
-            for h in range(TILES):
-                transpose_h_attn(k, h)
+        for h in range(TILES):
+            transpose_h_attn(0, h)
         quantise_h_attn(0)
+        quantise_w_out()
         first_matmul(0, 0)
-        for k in range(GROUPS + 4):
+        for h in range(TILES):
+            transpose_h_attn(1, h)
+        for k in range(GROUPS + 5):
             if k % 2 == 0 and k // 2 + LOADS_AHEAD < LOADS:
-                load(k // 2 + LOADS_AHEAD)
+                load_h_attn(k // 2 + LOADS_AHEAD)
+                load_x(k // 2 + LOADS_AHEAD)
             for h in range(TILES):
-                acc2 = second_matmul(k - 4, h) if live(k - 4) else None
+                acc2 = second_matmul(k - 5, h) if live(k - 5) else None
                 after_k, after_h = (k, 1) if h == 0 else (k + 1, 0)
                 if live(after_k):
                     first_matmul(after_k, after_h)
@@ -348,23 +363,26 @@ def tile_minitransformerlayer_pb_t_kernel(tc, h_attn, x, w_out, w_fc1, g2, b2, o
                     variance(before_k, before_h)
                 if live(k):
                     add_residual(k, h)
-                if live(k - 1):
-                    normalise(k - 1, h)
-                if live(k - 4):
-                    gelu(k - 4, h, acc2)
-                if h == 1 and live(k - 3):
-                    quantise_h(k - 3)
-                if live(k - 2):
-                    transpose_z(k - 2, h)
-                if h == 0 and live(k - 3):
-                    regroup_h(k - 3)
+                if h == 1 and live(k - 1):
+                    reciprocal_std(k - 1)
+                    normalise(k - 1, 0)
+                if h == 1 and live(k - 2):
+                    normalise(k - 2, 1)
+                if live(k - 5):
+                    gelu(k - 5, h, acc2)
+                if h == 1 and live(k - 4):
+                    quantise_h(k - 4)
+                if live(k - 3):
+                    transpose_z(k - 3, h)
+                if h == 0 and live(k - 4):
+                    regroup_h(k - 4)
                 if h == 0 and live(k + 1):
                     quantise_h_attn(k + 1)
                 if live(k + 2):
                     transpose_h_attn(k + 2, h)
                 if k == 0 and h == 0:
                     transpose_gain_and_bias()
-                if k == 0 and h == 1:
-                    quantise_w_fc1(0)
-                if k == 1 and h == 0:
-                    quantise_w_fc1(1)
+                if k == 1:
+                    transpose_w_fc1(h)
+                if k == 3:
+                    quantise_w_fc1(h)

@@ -44,8 +44,7 @@ def tile_minitransformerlayer_pb_t_kernel(tc, h_attn, x, w_out, w_fc1, g2, b2, o
         loads = ctx.enter_context(tc.tile_pool(name="loads", bufs=LOADS_AHEAD + 1))
         work = ctx.enter_context(tc.tile_pool(name="work", bufs=2))
         small = ctx.enter_context(tc.tile_pool(name="small", bufs=6))
-        s1p = ctx.enter_context(tc.psum_pool(name="s1p", bufs=4))
-        s2p = ctx.enter_context(tc.psum_pool(name="s2p", bufs=1))
+        accp = ctx.enter_context(tc.psum_pool(name="accp", bufs=5))
         ztp = ctx.enter_context(tc.psum_pool(name="ztp", bufs=2))
         htp = ctx.enter_context(tc.psum_pool(name="htp", bufs=1))
 
@@ -78,14 +77,14 @@ def tile_minitransformerlayer_pb_t_kernel(tc, h_attn, x, w_out, w_fc1, g2, b2, o
             nc.sync.dma_start(out=w1_raw_blocks[:, blocks, :], in_=w_out_blocks[:, blocks, :])
         load_x(0)
         load_h_attn(1)
+        load_h_attn(2)
+        load_x(1)
         gb_rows = const.tile([P, P], BF16)
         nc.vector.memset(gb_rows[:], 0.0)
         nc.sync.dma_start(out=gb_rows[0:D_BLOCKS, :], in_=g2.rearrange("(c p) -> c p", p=P))
         nc.sync.dma_start(out=gb_rows[D_BLOCKS : 2 * D_BLOCKS, :], in_=b2.rearrange("(c p) -> c p", p=P))
         w2_raw = const.tile([P, F // P, D], BF16)
         nc.sync.dma_start(out=w2_raw[:], in_=w_fc1.rearrange("(r p) k -> p r k", p=P))
-        load_x(1)
-        load_h_attn(2)
         load_x(2)
 
         ident_f32 = const.tile([P, P], F32)
@@ -128,24 +127,21 @@ def tile_minitransformerlayer_pb_t_kernel(tc, h_attn, x, w_out, w_fc1, g2, b2, o
         def transpose_gain_and_bias():
             gb_ps = ztp.tile([P, P], BF16, tag="ztp")
             nc.tensor.transpose(gb_ps[:], gb_rows[:], ident_bf[:])
-            nc.vector.tensor_copy(out=gb[:], in_=gb_ps[:, 0 : 2 * D_BLOCKS])
+            nc.scalar.copy(out=gb[:], in_=gb_ps[:, 0 : 2 * D_BLOCKS])
 
         w2_grp = const.tile([P, PASSES2, F, 4], BF16, align_bytes=64)
         w2_codes = const.tile([P, PASSES2, F], U32, align_bytes=64)
         w2_scales = const.tile([P, PASSES2, F], U8, align_bytes=64)
 
-        def transpose_w_fc1(s):
-            for q in range(F // P // 2):
-                w2_ps = ztp.tile([P, 4, 2 * P], BF16, tag="ztp")
-                for t in range(4):
-                    for rr in range(2):
-                        c = 4 * s + t
-                        nc.tensor.transpose(
-                            w2_ps[:, t, rr * P : (rr + 1) * P], w2_raw[:, 2 * q + rr, c * P : (c + 1) * P], ident_bf[:]
-                        )
-                nc.scalar.copy(
-                    out=w2_grp[:, s, q * 2 * P : (q + 1) * 2 * P, :], in_=w2_ps[:].rearrange("p t f -> p f t")
-                )
+        def transpose_w_fc1(s, q):
+            w2_ps = ztp.tile([P, 4, 2 * P], BF16, tag="ztp")
+            for t in range(4):
+                for rr in range(2):
+                    c = 4 * s + t
+                    nc.tensor.transpose(
+                        w2_ps[:, t, rr * P : (rr + 1) * P], w2_raw[:, 2 * q + rr, c * P : (c + 1) * P], ident_bf[:]
+                    )
+            nc.scalar.copy(out=w2_grp[:, s, q * 2 * P : (q + 1) * 2 * P, :], in_=w2_ps[:].rearrange("p t f -> p f t"))
 
         def quantise_w_fc1(s):
             nc.vector.quantize_mx(
@@ -179,15 +175,15 @@ def tile_minitransformerlayer_pb_t_kernel(tc, h_attn, x, w_out, w_fc1, g2, b2, o
                 col = ((k % 2) * TILES + h) * (E // 2) + u * P
                 nc.tensor.transpose(h_ps[:, u, h * P : (h + 1) * P], ha_words[:, col : col + P], ident_f32[:])
             if h == TILES - 1:
-                h_grp = work.tile([P, GROUP * 4], BF16, align_bytes=64, name="h_grp")
+                h_grp = work.tile([P, GROUP * 4], BF16, align_bytes=64, name="h_grp", bufs=3)
                 nc.scalar.copy(
                     out=h_grp[:].bitcast(F32).rearrange("p (r u) -> p r u", u=2), in_=h_ps[:].rearrange("p u r -> p r u")
                 )
                 h_groups[k] = h_grp
 
         def quantise_h_attn(k):
-            h_codes = work.tile([P, GROUP], U32, align_bytes=64, name="h_codes", bufs=3)
-            h_scales = work.tile([P, GROUP], U8, align_bytes=64, name="h_scales", bufs=3)
+            h_codes = work.tile([P, GROUP], U32, align_bytes=64, name="h_codes", bufs=4)
+            h_scales = work.tile([P, GROUP], U8, align_bytes=64, name="h_scales", bufs=4)
             nc.vector.quantize_mx(out=h_codes[:].bitcast(FP8X4), scales=h_scales[:], in_=h_groups[k][:])
             h_ops[k] = (h_codes, h_scales)
 
@@ -196,7 +192,7 @@ def tile_minitransformerlayer_pb_t_kernel(tc, h_attn, x, w_out, w_fc1, g2, b2, o
             tok = slice(h * P, (h + 1) * P)
             for half in range(D // BANK):
                 cols = slice(half * BANK, (half + 1) * BANK)
-                acc1 = s1p.tile([P, BANK], F32, name="acc1")
+                acc1 = accp.tile([P, BANK], F32, tag="acc")
                 nc.tensor.matmul_mx(
                     out=acc1[:],
                     lhsT=h_codes[:, tok].bitcast(FP8X4),
@@ -208,27 +204,31 @@ def tile_minitransformerlayer_pb_t_kernel(tc, h_attn, x, w_out, w_fc1, g2, b2, o
                 )
                 acc1_banks[(k, h, half)] = acc1
 
-        def add_residual(k, h):
-            if h == 0:
+        def add_residual(k, h, half):
+            if h == 0 and half == 0:
                 xm_tiles[k] = work.tile([P, TILES, D], F32, name="xm", bufs=4)
                 mean_tiles[k] = (
                     small.tile([P, TILES, 2], F32, name="sums"),
                     small.tile([P, TILES], F32, name="neg_mu"),
                 )
             xm = xm_tiles[k]
-            sums, neg_mu = mean_tiles[k]
+            sums = mean_tiles[k][0]
             x_sb = x_tiles[k // 2]
-            for half in range(D // BANK):
-                cols = slice(half * BANK, (half + 1) * BANK)
-                nc.vector.scalar_tensor_tensor(
-                    out=xm[:, h, cols],
-                    in0=acc1_banks[(k, h, half)][:],
-                    scalar=1.0,
-                    in1=x_sb[:, (k % 2) * TILES + h, cols],
-                    op0=ALU.mult,
-                    op1=ALU.add,
-                    accum_out=sums[:, h, half : half + 1],
-                )
+            cols = slice(half * BANK, (half + 1) * BANK)
+            nc.vector.scalar_tensor_tensor(
+                out=xm[:, h, cols],
+                in0=acc1_banks[(k, h, half)][:],
+                scalar=1.0,
+                in1=x_sb[:, (k % 2) * TILES + h, cols],
+                op0=ALU.mult,
+                op1=ALU.add,
+                accum_out=sums[:, h, half : half + 1],
+            )
+            if h == TILES - 1 and half == 1:
+                nc.sync.dma_start(out=group_view(xmid_rows, k), in_=xm[:])
+
+        def minus_mean(k, h):
+            sums, neg_mu = mean_tiles[k]
             nc.vector.tensor_scalar(
                 out=neg_mu[:, h : h + 1],
                 in0=sums[:, h, 0:1],
@@ -237,8 +237,6 @@ def tile_minitransformerlayer_pb_t_kernel(tc, h_attn, x, w_out, w_fc1, g2, b2, o
                 op0=ALU.add,
                 op1=ALU.mult,
             )
-            if h == TILES - 1:
-                nc.sync.dma_start(out=group_view(xmid_rows, k), in_=xm[:])
 
         def variance(k, h):
             if h == 0:
@@ -299,18 +297,17 @@ def tile_minitransformerlayer_pb_t_kernel(tc, h_attn, x, w_out, w_fc1, g2, b2, o
                             out=planes[:, c, :], in_=z_ps[:, cc, :], func=ACT.Identity, bias=shift, scale=gain
                         )
 
-        def regroup_h(k):
-            z_grp = work.tile([P, PASSES2, GROUP, 4], BF16, align_bytes=64, name="z_grp")
-            for s in range(PASSES2):
-                nc.vector.tensor_copy(
-                    out=z_grp[:, s, :, :].rearrange("p (c i) t -> p c t i", i=4),
-                    in_=plane_tiles[k][:, 4 * s : 4 * s + 4, :].rearrange("p t (c i) -> p c t i", i=4),
-                )
-            zgrp_tiles[k] = z_grp
+        def regroup_h(k, s):
+            if s == 0:
+                zgrp_tiles[k] = work.tile([P, PASSES2, GROUP, 4], BF16, align_bytes=64, name="z_grp")
+            nc.vector.tensor_copy(
+                out=zgrp_tiles[k][:, s, :, :].rearrange("p (c i) t -> p c t i", i=4),
+                in_=plane_tiles[k][:, 4 * s : 4 * s + 4, :].rearrange("p t (c i) -> p c t i", i=4),
+            )
 
         def quantise_h(k):
-            z_codes = work.tile([P, PASSES2, GROUP], U32, align_bytes=64, name="z_codes")
-            z_scales = work.tile([P, PASSES2, GROUP], U8, align_bytes=64, name="z_scales")
+            z_codes = work.tile([P, PASSES2, GROUP], U32, align_bytes=64, name="z_codes", bufs=3)
+            z_scales = work.tile([P, PASSES2, GROUP], U8, align_bytes=64, name="z_scales", bufs=3)
             nc.vector.quantize_mx(
                 out=z_codes[:].rearrange("p s r -> p (s r)").bitcast(FP8X4),
                 scales=z_scales[:].rearrange("p s r -> p (s r)"),
@@ -321,7 +318,7 @@ def tile_minitransformerlayer_pb_t_kernel(tc, h_attn, x, w_out, w_fc1, g2, b2, o
         def second_matmul(k, h):
             z_codes, z_scales = z_ops[k]
             tok = slice(h * P, (h + 1) * P)
-            acc2 = s2p.tile([P, F], F32, name="acc2")
+            acc2 = accp.tile([P, F], F32, tag="acc")
             for s in range(PASSES2):
                 nc.tensor.matmul_mx(
                     out=acc2[:],
@@ -346,43 +343,55 @@ def tile_minitransformerlayer_pb_t_kernel(tc, h_attn, x, w_out, w_fc1, g2, b2, o
             transpose_h_attn(0, h)
         quantise_h_attn(0)
         quantise_w_out()
-        first_matmul(0, 0)
         for h in range(TILES):
             transpose_h_attn(1, h)
-        for k in range(GROUPS + 5):
+        first_matmul(0, 0)
+        for h in range(TILES):
+            transpose_h_attn(2, h)
+        for k in range(GROUPS + 6):
             if k % 2 == 0 and k // 2 + LOADS_AHEAD < LOADS:
                 load_h_attn(k // 2 + LOADS_AHEAD)
                 load_x(k // 2 + LOADS_AHEAD)
             for h in range(TILES):
-                acc2 = second_matmul(k - 5, h) if live(k - 5) else None
+                acc2 = second_matmul(k - 6, h) if live(k - 6) else None
                 after_k, after_h = (k, 1) if h == 0 else (k + 1, 0)
                 if live(after_k):
                     first_matmul(after_k, after_h)
+                if live(k):
+                    add_residual(k, h, 0)
+                    if h == 1:
+                        minus_mean(k, 0)
+                    add_residual(k, h, 1)
+                if k == 0 and h == 0:
+                    quantise_h_attn(1)
                 before_k, before_h = (k - 1, 1) if h == 0 else (k, 0)
                 if live(before_k):
                     variance(before_k, before_h)
-                if live(k):
-                    add_residual(k, h)
-                if h == 1 and live(k - 1):
-                    reciprocal_std(k - 1)
-                    normalise(k - 1, 0)
-                if h == 1 and live(k - 2):
-                    normalise(k - 2, 1)
-                if live(k - 5):
-                    gelu(k - 5, h, acc2)
-                if h == 1 and live(k - 4):
-                    quantise_h(k - 4)
+                if live(k - 6):
+                    gelu(k - 6, h, acc2)
+                if h == 1:
+                    if live(k - 4):
+                        regroup_h(k - 4, 0)
+                    if live(k):
+                        minus_mean(k, 1)
+                    if live(k - 4):
+                        regroup_h(k - 4, 1)
+                    if live(k + 2):
+                        quantise_h_attn(k + 2)
+                    if live(k - 2):
+                        normalise(k - 2, 1)
+                    if live(k - 4):
+                        quantise_h(k - 4)
+                    if live(k - 1):
+                        reciprocal_std(k - 1)
+                        normalise(k - 1, 0)
                 if live(k - 3):
                     transpose_z(k - 3, h)
-                if h == 0 and live(k - 4):
-                    regroup_h(k - 4)
-                if h == 0 and live(k + 1):
-                    quantise_h_attn(k + 1)
-                if live(k + 2):
-                    transpose_h_attn(k + 2, h)
-                if k == 0 and h == 0:
+                if live(k + 3):
+                    transpose_h_attn(k + 3, h)
+                if k == 1 and h == 1:
                     transpose_gain_and_bias()
-                if k == 1:
-                    transpose_w_fc1(h)
-                if k == 3:
+                if k == 2 or k == 3:
+                    transpose_w_fc1(k - 2, h)
+                if k == 5:
                     quantise_w_fc1(h)

@@ -263,8 +263,7 @@ def tile_minitransformerlayer_pb_t_kernel(tc, h_attn, x, w_out, w_fc1, g2, b2, o
             if h == 0:
                 z_tiles[k] = work.tile([P, TILES, D], F32, name="z", bufs=4)
             one = slice(h, h + 1)
-            engine = nc.gpsimd if h == 0 else nc.vector
-            engine.tensor_scalar(
+            nc.gpsimd.tensor_scalar(
                 out=z_tiles[k][:, h, :],
                 in0=xm_tiles[k][:, h, :],
                 scalar1=mean_tiles[k][1][:, one],
@@ -378,13 +377,12 @@ def tile_minitransformerlayer_pb_t_kernel(tc, h_attn, x, w_out, w_fc1, g2, b2, o
                         regroup_h(k - 4, 1)
                     if live(k + 2):
                         quantise_h_attn(k + 2)
-                    if live(k - 2):
-                        normalise(k - 2, 1)
                     if live(k - 4):
                         quantise_h(k - 4)
                     if live(k - 1):
                         reciprocal_std(k - 1)
                         normalise(k - 1, 0)
+                        normalise(k - 1, 1)
                 if live(k - 3):
                     transpose_z(k - 3, h)
                 if live(k + 3):

@@ -287,7 +287,7 @@ def tile_minitransformerlayer_pb_t_kernel(tc, h_attn, x, w_out, w_fc1, g2, b2, o
                     c = 4 * h + 2 * b + cc
                     gain = gb[:, c : c + 1]
                     shift = gb[:, D_BLOCKS + c : D_BLOCKS + c + 1]
-                    if h == 1 and b == 1:
+                    if h == 1 and (b == 1 or k % 2 == 1):
                         nc.vector.tensor_scalar(
                             out=planes[:, c, :], in0=z_ps[:, cc, :], scalar1=gain, scalar2=shift, op0=ALU.mult, op1=ALU.add
                         )

from contextlib import ExitStack

import concourse.mybir as mybir
from concourse.masks import make_identity

F32 = mybir.dt.float32
BF16 = mybir.dt.bfloat16
U32 = mybir.dt.uint32
U8 = mybir.dt.uint8
FP8X4 = mybir.dt.float8_e4m3fn_x4
ACT = mybir.ActivationFunctionType
ALU = mybir.AluOpType

P = 128
TOKENS = 4096
D = 1024
E = 512
F = 512
EPS = 1e-5
BANK = 512
D_BLOCKS = D // P
PASSES2 = D // 512
LOAD_TILES = 4
LOAD_TOKENS = LOAD_TILES * P
LOADS = TOKENS // LOAD_TOKENS
TILES = 2
GROUP = TILES * P
GROUPS = TOKENS // GROUP
LOADS_AHEAD = 3

FLOPS = 2 * TOKENS * E * D + 2 * TOKENS * D * F


def tile_minitransformerlayer_pb_t_kernel(tc, h_attn, x, w_out, w_fc1, g2, b2, out_0, out_1):
    nc = tc.nc
    ha_rows = h_attn.flatten_outer_dims()
    x_rows = x.flatten_outer_dims()
    xmid_rows = out_0.flatten_outer_dims()
    act_rows = out_1.flatten_outer_dims()

    with ExitStack() as ctx:
        ctx.enter_context(tc.manual_schedule())
        const = ctx.enter_context(tc.tile_pool(name="const", bufs=1))
        loads = ctx.enter_context(tc.tile_pool(name="loads", bufs=LOADS_AHEAD + 1))
        work = ctx.enter_context(tc.tile_pool(name="work", bufs=2))
        small = ctx.enter_context(tc.tile_pool(name="small", bufs=6))
        accp = ctx.enter_context(tc.psum_pool(name="accp", bufs=5))
        ztp = ctx.enter_context(tc.psum_pool(name="ztp", bufs=2))
        htp = ctx.enter_context(tc.psum_pool(name="htp", bufs=1))

        def load_view(rows, n):
            return rows[n * LOAD_TOKENS : (n + 1) * LOAD_TOKENS, :].rearrange("(p j) c -> p j c", j=LOAD_TILES)

        def group_view(rows, k):
            first = (k % 2) * TILES
            return load_view(rows, k // 2)[:, first : first + TILES, :]

        ha_tiles = {}
        x_tiles = {}

        def load_h_attn(n):
            ha_sb = loads.tile([P, LOAD_TILES * E], BF16, name="ha_sb")
            nc.sync.dma_start(out=ha_sb[:].rearrange("p (j c) -> p j c", j=LOAD_TILES), in_=load_view(ha_rows, n))
            ha_tiles[n] = ha_sb

        def load_x(n):
            x_sb = loads.tile([P, LOAD_TILES, D], BF16, name="x_sb")
            nc.sync.dma_start(out=x_sb[:], in_=load_view(x_rows, n))
            x_tiles[n] = x_sb

        load_h_attn(0)
        w1_raw = const.tile([P, D_BLOCKS * E], BF16)
        w1_raw_blocks = w1_raw[:].rearrange("p (r k) -> p r k", k=E)
        w_out_blocks = w_out.rearrange("(r p) k -> p r k", p=P)
        for half in range(D // BANK):
            blocks = slice(half * BANK // P, (half + 1) * BANK // P)
            nc.sync.dma_start(out=w1_raw_blocks[:, blocks, :], in_=w_out_blocks[:, blocks, :])
        load_x(0)
        load_h_attn(1)
        load_h_attn(2)
        load_x(1)
        gb_rows = const.tile([P, P], BF16)
        nc.vector.memset(gb_rows[:], 0.0)
        nc.sync.dma_start(out=gb_rows[0:D_BLOCKS, :], in_=g2.rearrange("(c p) -> c p", p=P))
        nc.sync.dma_start(out=gb_rows[D_BLOCKS : 2 * D_BLOCKS, :], in_=b2.rearrange("(c p) -> c p", p=P))
        w2_raw = const.tile([P, F // P, D], BF16)
        nc.sync.dma_start(out=w2_raw[:], in_=w_fc1.rearrange("(r p) k -> p r k", p=P))
        load_x(2)

        ident_f32 = const.tile([P, P], F32)
        make_identity(nc, ident_f32[:])
        ident_bf = const.tile([P, P], BF16)
        make_identity(nc, ident_bf[:])
        neg_half = const.tile([P, TILES], F32)
        nc.gpsimd.memset(neg_half[:], -0.5)
        warm = const.tile([P, 1], F32)
        nc.vector.memset(warm[:], 0.0)
        nc.scalar.activation(out=warm[:], in_=warm[:], func=ACT.Gelu)

        w1_grp = const.tile([P, D * 4], BF16, align_bytes=64)
        w1_grp_words = w1_grp[:].bitcast(F32).rearrange("p (d u) -> p d u", u=2)
        w1_words = w1_raw[:].bitcast(F32)
        w1_codes = const.tile([P, D], U32, align_bytes=64)
        w1_scales = const.tile([P, D], U8, align_bytes=64)

        def quantise_w_out():
            for q in range(D_BLOCKS // 2):
                w1_ps = ztp.tile([P, 2, 2 * P], F32, tag="ztp")
                for rr in range(2):
                    for u in range(2):
                        col = (2 * q + rr) * (E // 2) + u * P
                        nc.tensor.transpose(w1_ps[:, u, rr * P : (rr + 1) * P], w1_words[:, col : col + P], ident_f32[:])
                w1_out = w1_grp_words[:, q * 2 * P : (q + 1) * 2 * P, :]
                if q % 2 == 0:
                    nc.vector.tensor_copy(out=w1_out, in_=w1_ps[:].rearrange("p u d -> p d u"))
                else:
                    nc.scalar.copy(out=w1_out, in_=w1_ps[:].rearrange("p u d -> p d u"))
                    half = q // 2
                    nc.vector.quantize_mx(
                        out=w1_codes[:, half * BANK : (half + 1) * BANK].bitcast(FP8X4),
                        scales=w1_scales[:, half * BANK : (half + 1) * BANK],
                        in_=w1_grp[:, half * BANK * 4 : (half + 1) * BANK * 4],
                    )

        gb = const.tile([P, 2 * D_BLOCKS], F32)

        def transpose_gain_and_bias():
            gb_ps = ztp.tile([P, P], BF16, tag="ztp")
            nc.tensor.transpose(gb_ps[:], gb_rows[:], ident_bf[:])
            nc.scalar.copy(out=gb[:], in_=gb_ps[:, 0 : 2 * D_BLOCKS])

        w2_grp = const.tile([P, PASSES2, F, 4], BF16, align_bytes=64)
        w2_codes = const.tile([P, PASSES2, F], U32, align_bytes=64)
        w2_scales = const.tile([P, PASSES2, F], U8, align_bytes=64)

        def transpose_w_fc1(s, q):
            w2_ps = ztp.tile([P, 4, 2 * P], BF16, tag="ztp")
            for t in range(4):
                for rr in range(2):
                    c = 4 * s + t
                    nc.tensor.transpose(
                        w2_ps[:, t, rr * P : (rr + 1) * P], w2_raw[:, 2 * q + rr, c * P : (c + 1) * P], ident_bf[:]
                    )
            nc.scalar.copy(out=w2_grp[:, s, q * 2 * P : (q + 1) * 2 * P, :], in_=w2_ps[:].rearrange("p t f -> p f t"))

        def quantise_w_fc1(s):
            nc.vector.quantize_mx(
                out=w2_codes[:, s, :].bitcast(FP8X4),
                scales=w2_scales[:, s, :],
                in_=w2_grp[:, s, :, :].rearrange("p f t -> p (f t)"),
            )

        h_banks = {}
        h_groups = {}
        h_ops = {}
        acc1_banks = {}
        xm_tiles = {}
        mean_tiles = {}
        z_tiles = {}
        norm_tiles = {}
        plane_tiles = {}
        zgrp_tiles = {}
        z_ops = {}
        act_tiles = {}

        def live(k):
            return 0 <= k < GROUPS

        def transpose_h_attn(k, h):
            if h == 0:
                h_banks[k] = htp.tile([P, 2, GROUP], F32, name="h_ps")
            h_ps = h_banks[k]
            ha_words = ha_tiles[k // 2][:].bitcast(F32)
            for u in range(2):
                col = ((k % 2) * TILES + h) * (E // 2) + u * P
                nc.tensor.transpose(h_ps[:, u, h * P : (h + 1) * P], ha_words[:, col : col + P], ident_f32[:])
            if h == TILES - 1:
                h_grp = work.tile([P, GROUP * 4], BF16, align_bytes=64, name="h_grp", bufs=3)
                nc.scalar.copy(
                    out=h_grp[:].bitcast(F32).rearrange("p (r u) -> p r u", u=2), in_=h_ps[:].rearrange("p u r -> p r u")
                )
                h_groups[k] = h_grp

        def quantise_h_attn(k):
            h_codes = work.tile([P, GROUP], U32, align_bytes=64, name="h_codes", bufs=4)
            h_scales = work.tile([P, GROUP], U8, align_bytes=64, name="h_scales", bufs=4)
            nc.vector.quantize_mx(out=h_codes[:].bitcast(FP8X4), scales=h_scales[:], in_=h_groups[k][:])
            h_ops[k] = (h_codes, h_scales)

        def first_matmul(k, h):
            h_codes, h_scales = h_ops[k]
            tok = slice(h * P, (h + 1) * P)
            for half in range(D // BANK):
                cols = slice(half * BANK, (half + 1) * BANK)
                acc1 = accp.tile([P, BANK], F32, tag="acc")
                nc.tensor.matmul_mx(
                    out=acc1[:],
                    lhsT=h_codes[:, tok].bitcast(FP8X4),
                    lhsT_scale=h_scales[:, tok],
                    rhs=w1_codes[:, cols].bitcast(FP8X4),
                    rhs_scale=w1_scales[:, cols],
                    start=True,
                    stop=True,
                )
                acc1_banks[(k, h, half)] = acc1

        def add_residual(k, h, half):
            if h == 0 and half == 0:
                xm_tiles[k] = work.tile([P, TILES, D], F32, name="xm", bufs=4)
                mean_tiles[k] = (
                    small.tile([P, TILES, 2], F32, name="sums"),
                    small.tile([P, TILES], F32, name="neg_mu"),
                )
            xm = xm_tiles[k]
            sums = mean_tiles[k][0]
            x_sb = x_tiles[k // 2]
            cols = slice(half * BANK, (half + 1) * BANK)
            nc.vector.scalar_tensor_tensor(
                out=xm[:, h, cols],
                in0=acc1_banks[(k, h, half)][:],
                scalar=1.0,
                in1=x_sb[:, (k % 2) * TILES + h, cols],
                op0=ALU.mult,
                op1=ALU.add,
                accum_out=sums[:, h, half : half + 1],
            )
            if h == TILES - 1 and half == 1:
                nc.sync.dma_start(out=group_view(xmid_rows, k), in_=xm[:])

        def minus_mean(k, h):
            sums, neg_mu = mean_tiles[k]
            nc.vector.tensor_scalar(
                out=neg_mu[:, h : h + 1],
                in0=sums[:, h, 0:1],
                scalar1=sums[:, h, 1:2],
                scalar2=-1.0 / D,
                op0=ALU.add,
                op1=ALU.mult,
            )

        def variance(k, h):
            if h == 0:
                norm_tiles[k] = (
                    small.tile([P, TILES], F32, name="ssq"),
                    small.tile([P, TILES], F32, name="var_eps"),
                    small.tile([P, TILES], F32, name="rstd"),
                )
            xm = xm_tiles[k]
            neg_mu = mean_tiles[k][1]
            ssq, var_eps, rstd = norm_tiles[k]
            one = slice(h, h + 1)
            squares = work.tile([P, D], BF16, name="squares")
            nc.scalar.activation(
                out=squares[:], in_=xm[:, h, :], func=ACT.Square, bias=neg_mu[:, one], scale=1.0, accum_out=ssq[:, one]
            )

        def reciprocal_std(k):
            ssq, var_eps, rstd = norm_tiles[k]
            nc.vector.tensor_scalar(out=var_eps[:], in0=ssq[:], scalar1=1.0 / D, scalar2=EPS, op0=ALU.mult, op1=ALU.add)
            nc.gpsimd.tensor_tensor(out=rstd[:], in0=var_eps[:], in1=neg_half[:], op=ALU.pow)

        def normalise(k, h):
            if h == 0:
                z_tiles[k] = work.tile([P, TILES, D], F32, name="z", bufs=4)
            one = slice(h, h + 1)
            nc.gpsimd.tensor_scalar(
                out=z_tiles[k][:, h, :],
                in0=xm_tiles[k][:, h, :],
                scalar1=mean_tiles[k][1][:, one],
                scalar2=norm_tiles[k][2][:, one],
                op0=ALU.add,
                op1=ALU.mult,
            )

        def transpose_z(k, h):
            if h == 0:
                plane_tiles[k] = work.tile([P, D_BLOCKS, GROUP], BF16, name="planes")
            planes = plane_tiles[k]
            z = z_tiles[k]
            for b in range(2):
                z_ps = ztp.tile([P, 2, GROUP], F32, tag="ztp")
                for cc in range(2):
                    c = 4 * h + 2 * b + cc
                    for j in range(TILES):
                        nc.tensor.transpose(z_ps[:, cc, j * P : (j + 1) * P], z[:, j, c * P : (c + 1) * P], ident_f32[:])
                for cc in range(2):
                    c = 4 * h + 2 * b + cc
                    gain = gb[:, c : c + 1]
                    shift = gb[:, D_BLOCKS + c : D_BLOCKS + c + 1]
                    if h == 1 and (b == 1 or k % 2 == 1):
                        nc.vector.tensor_scalar(
                            out=planes[:, c, :], in0=z_ps[:, cc, :], scalar1=gain, scalar2=shift, op0=ALU.mult, op1=ALU.add
                        )
                    else:
                        nc.scalar.activation(
                            out=planes[:, c, :], in_=z_ps[:, cc, :], func=ACT.Identity, bias=shift, scale=gain
                        )

        def regroup_h(k, s):
            if s == 0:
                zgrp_tiles[k] = work.tile([P, PASSES2, GROUP, 4], BF16, align_bytes=64, name="z_grp")
            nc.vector.tensor_copy(
                out=zgrp_tiles[k][:, s, :, :].rearrange("p (c i) t -> p c t i", i=4),
                in_=plane_tiles[k][:, 4 * s : 4 * s + 4, :].rearrange("p t (c i) -> p c t i", i=4),
            )

        def quantise_h(k):
            z_codes = work.tile([P, PASSES2, GROUP], U32, align_bytes=64, name="z_codes", bufs=3)
            z_scales = work.tile([P, PASSES2, GROUP], U8, align_bytes=64, name="z_scales", bufs=3)
            nc.vector.quantize_mx(
                out=z_codes[:].rearrange("p s r -> p (s r)").bitcast(FP8X4),
                scales=z_scales[:].rearrange("p s r -> p (s r)"),
                in_=zgrp_tiles[k][:].rearrange("p s r t -> p (s r t)"),
            )
            z_ops[k] = (z_codes, z_scales)

        def second_matmul(k, h):
            z_codes, z_scales = z_ops[k]
            tok = slice(h * P, (h + 1) * P)
            acc2 = accp.tile([P, F], F32, tag="acc")
            for s in range(PASSES2):
                nc.tensor.matmul_mx(
                    out=acc2[:],
                    lhsT=z_codes[:, s, tok].bitcast(FP8X4),
                    lhsT_scale=z_scales[:, s, tok],
                    rhs=w2_codes[:, s, :].bitcast(FP8X4),
                    rhs_scale=w2_scales[:, s, :],
                    start=(s == 0),
                    stop=(s == PASSES2 - 1),
                )
            return acc2

        def gelu(k, h, acc2):
            if h == 0:
                act_tiles[k] = work.tile([P, TILES, F], F32, name="act", bufs=3)
            act = act_tiles[k]
            nc.scalar.activation(out=act[:, h, :], in_=acc2[:], func=ACT.Gelu)
            if h == TILES - 1:
                nc.sync.dma_start(out=group_view(act_rows, k), in_=act[:])

        for h in range(TILES):
            transpose_h_attn(0, h)
        quantise_h_attn(0)
        quantise_w_out()
        for h in range(TILES):
            transpose_h_attn(1, h)
        first_matmul(0, 0)
        for h in range(TILES):
            transpose_h_attn(2, h)
        for k in range(GROUPS + 6):
            if k % 2 == 0 and k // 2 + LOADS_AHEAD < LOADS:
                load_h_attn(k // 2 + LOADS_AHEAD)
                load_x(k // 2 + LOADS_AHEAD)
            for h in range(TILES):
                acc2 = second_matmul(k - 6, h) if live(k - 6) else None
                after_k, after_h = (k, 1) if h == 0 else (k + 1, 0)
                if live(after_k):
                    first_matmul(after_k, after_h)
                if live(k):
                    add_residual(k, h, 0)
                    if h == 1:
                        minus_mean(k, 0)
                    add_residual(k, h, 1)
                if k == 0 and h == 0:
                    quantise_h_attn(1)
                before_k, before_h = (k - 1, 1) if h == 0 else (k, 0)
                if live(before_k):
                    variance(before_k, before_h)
                if live(k - 6):
                    gelu(k - 6, h, acc2)
                if h == 1:
                    if live(k - 4):
                        regroup_h(k - 4, 0)
                    if live(k):
                        minus_mean(k, 1)
                    if live(k - 4):
                        regroup_h(k - 4, 1)
                    if live(k + 2):
                        quantise_h_attn(k + 2)
                    if live(k - 4):
                        quantise_h(k - 4)
                    if live(k - 1):
                        reciprocal_std(k - 1)
                        normalise(k - 1, 0)
                        normalise(k - 1, 1)
                if live(k - 3):
                    transpose_z(k - 3, h)
                if live(k + 3):
                    transpose_h_attn(k + 3, h)
                if k == 1 and h == 1:
                    transpose_gain_and_bias()
                if k == 2 or k == 3:
                    transpose_w_fc1(k - 2, h)
                if k == 5:
                    quantise_w_fc1(h)
